import numpy as np
import ml_dtypes


def mxq(x, axis, fmt="e4m3"):
    dtype, down = {"e4m3": (ml_dtypes.float8_e4m3fn, 7), "e5m2": (ml_dtypes.float8_e5m2, 14)}[fmt]
    v = np.moveaxis(np.asarray(x, np.float32).astype(ml_dtypes.bfloat16).astype(np.float64), axis, -1)
    blocks = v.reshape(v.shape[:-1] + (-1, 32))
    amax = np.abs(blocks).max(-1, keepdims=True)
    byte = np.maximum(np.where(amax > 0, np.frexp(amax)[1] - 1 + 127, 0) - down, 1)
    scale = np.exp2(byte - 127.0)
    codes = (blocks / scale).astype(np.float32).astype(dtype).astype(np.float64)
    return np.moveaxis((codes * scale).reshape(v.shape), -1, axis)


WIDE = False


def mx_kscale(k):
    if not WIDE:
        return np.ones(k)
    levels = np.array([10, -10, 5, -5, 0])
    a = np.random.permutation(np.resize(levels, k // 512 * 4)).reshape(k // 512, 4)
    idx = np.arange(k)
    return np.exp2(a[idx // 512, idx % 128 // 32])


BF16 = ml_dtypes.bfloat16


def bf(x):
    return np.asarray(x, np.float32).astype(BF16)


def f64(x):
    return np.asarray(x).astype(np.float64)


E2M1 = np.array([0.0, 0.5, 1.0, 1.5, 2.0, 3.0, 4.0, 6.0, -0.0, -0.5, -1.0, -1.5, -2.0, -3.0, -4.0, -6.0])


def pack_weight(w, fmt):
    k, n = w.shape
    w = f64(bf(w)).reshape(k // 32, 32, n)
    amax = np.abs(w).max(1)
    if fmt == "e4m3":
        byte = np.frexp(amax)[1] - 1 + 127 - 7
    else:
        mant, ex = np.frexp(amax / 6.0)
        byte = np.where(mant > 0.5, ex, ex - 1) + 127
    byte = np.clip(np.where(amax > 0, byte, 1), 1, 254)
    scaled = (w * np.exp2(127.0 - byte)[:, None, :]).reshape(k, n).astype(np.float32)
    by_word = np.ascontiguousarray(scaled.reshape(k // 512, 128, 4, n).transpose(0, 1, 3, 2))
    if fmt == "e4m3":
        words = by_word.astype(ml_dtypes.float8_e4m3fn).view(np.uint8)
    else:
        c = by_word.astype(ml_dtypes.float4_e2m1fn).view(np.uint8) & 0xF
        words = c[..., 0::2] | (c[..., 1::2] << 4)
    return np.ascontiguousarray(words), np.ascontiguousarray(byte.astype(np.uint8).reshape(k // 512, 16, n))


def unpack_weight(words, scales, fmt):
    g, p, n, _ = words.shape
    if fmt == "e4m3":
        vals = np.ascontiguousarray(words).view(ml_dtypes.float8_e4m3fn).astype(np.float64)
    else:
        nib = np.empty((g, p, n, 4), np.uint8)
        nib[..., 0::2] = words & 0xF
        nib[..., 1::2] = words >> 4
        vals = E2M1[nib]
    vals = vals * np.repeat(np.exp2(scales.astype(np.float64) - 127.0), 8, axis=1)[..., None]
    return vals.transpose(0, 1, 3, 2).reshape(g * 512, n)


B, S, E, P, H = 2, 512, 1024, 1024, 8
D = P // H
FMT = "e4m3"


def rope(x):
    inv_freq = 1.0 / (10000.0 ** (f64(np.arange(0, D, 2)) / D))
    t = f64(np.arange(S))
    freqs = np.repeat(t[:, None] * inv_freq[None, :], 2, axis=-1)
    cos, sin = np.cos(freqs), np.sin(freqs)
    xp = x.reshape(*x.shape[:-1], D // 2, 2)
    rot = np.stack((-xp[..., 1], xp[..., 0]), axis=-1).reshape(x.shape)
    return x * cos + rot * sin


def setup_inputs():
    s = mx_kscale(E)
    emb = bf(np.random.standard_normal((B, S, E)) * s)
    W1_words, W1_scales = pack_weight((np.random.standard_normal((P, E)) * 0.6 / np.sqrt(E) / s).T, FMT)
    W2_words, W2_scales = pack_weight((np.random.standard_normal((P, E)) * 0.6 / np.sqrt(E) / s).T, FMT)
    W3_words, W3_scales = pack_weight((np.random.standard_normal((P, E)) * 2.0 / np.sqrt(E) / s).T, FMT)
    return {"emb": emb,
            "W1_words": W1_words, "W1_scales": W1_scales,
            "W2_words": W2_words, "W2_scales": W2_scales,
            "W3_words": W3_words, "W3_scales": W3_scales}


def reference(emb, W1_words, W1_scales, W2_words, W2_scales, W3_words, W3_scales):
    xq = mxq(f64(emb), 2, "e4m3")
    q = (xq @ unpack_weight(W1_words, W1_scales, FMT)).reshape(B, H, S, D)
    k = (xq @ unpack_weight(W2_words, W2_scales, FMT)).reshape(B, H, S, D)
    v = (xq @ unpack_weight(W3_words, W3_scales, FMT)).reshape(B, H, S, D)
    return rope(q), rope(k), v

@@ -1,0 +1,234 @@
+import math
+from contextlib import ExitStack
+
+import concourse.mybir as mybir
+from concourse.masks import make_identity
+
+F32 = mybir.dt.float32
+BF16 = mybir.dt.bfloat16
+I32 = mybir.dt.int32
+U32 = mybir.dt.uint32
+U8 = mybir.dt.uint8
+FP8X4 = mybir.dt.float8_e4m3fn_x4
+ALU = mybir.AluOpType
+SIN = mybir.ActivationFunctionType.Sin
+
+P = 128
+PACK = 4
+K_PASS = P * PACK
+TOKENS = 1024
+FEATURES_IN = 1024
+FEATURES_OUT = 1024
+PASSES = FEATURES_IN // K_PASS
+TOKEN_TILES = TOKENS // P
+BANK = 512
+BANKS = FEATURES_OUT // BANK
+HEAD_DIM = 128
+CHUNKS = FEATURES_OUT // HEAD_DIM
+PAIRS = HEAD_DIM // 2
+ROW_PAIRS = FEATURES_OUT // 2
+BANK_PAIRS = BANK // 2
+ROTATED = 2
+WEIGHTS = 3
+QUADRANTS = 4
+PLANES_PER_TILE = 4
+
+FREQ_RATIO = 10000.0 ** (-2.0 / HEAD_DIM)
+DOUBLINGS = 6
+ROUND_TO_WHOLE = 1.5 * 2.0**23
+
+assert 2**DOUBLINGS == PAIRS
+
+FLOPS = 2 * TOKENS * FEATURES_IN * WEIGHTS * FEATURES_OUT
+
+
+def build_rotary_tables(nc, scratch, cos, sin, neg_sin):
+    position = scratch.tile([P, CHUNKS], F32)
+    for half in range(2):
+        nc.gpsimd.iota(
+            position[64 * half : 64 * half + 64, :],
+            pattern=[[1, CHUNKS]],
+            base=0,
+            channel_multiplier=CHUNKS,
+            allow_small_or_imprecise_dtypes=True,
+        )
+
+    turns = scratch.tile([P, CHUNKS, PAIRS], F32)
+    nc.vector.tensor_scalar_mul(
+        out=turns[:, :, 0:1], in0=position[:].unsqueeze(2), scalar1=1.0 / (2.0 * math.pi)
+    )
+    for step in range(DOUBLINGS):
+        width = 2**step
+        nc.vector.tensor_scalar_mul(
+            out=turns[:, :, width : 2 * width],
+            in0=turns[:, :, 0:width],
+            scalar1=FREQ_RATIO**width,
+        )
+    turns_flat = turns[:].rearrange("p c i -> p (c i)")
+
+    whole = scratch.tile([P, ROW_PAIRS], F32)
+    nc.vector.tensor_scalar(
+        out=whole[:],
+        in0=turns_flat,
+        scalar1=ROUND_TO_WHOLE,
+        scalar2=ROUND_TO_WHOLE,
+        op0=ALU.add,
+        op1=ALU.subtract,
+    )
+    part = scratch.tile([P, ROW_PAIRS], F32)
+    nc.vector.tensor_tensor(out=part[:], in0=turns_flat, in1=whole[:], op=ALU.subtract)
+    nc.scalar.activation(out=sin[:], in_=part[:], func=SIN, scale=2.0 * math.pi)
+    nc.scalar.activation(out=neg_sin[:], in_=part[:], func=SIN, scale=-2.0 * math.pi)
+
+    neg_abs = scratch.tile([P, ROW_PAIRS], F32)
+    nc.vector.scalar_tensor_tensor(
+        out=neg_abs[:], in0=part[:], scalar=-1.0, in1=part[:], op0=ALU.mult, op1=ALU.min
+    )
+    quarter_less = scratch.tile([P, ROW_PAIRS], F32)
+    nc.vector.tensor_scalar_add(out=quarter_less[:], in0=neg_abs[:], scalar1=0.25)
+    nc.scalar.activation(out=cos[:], in_=quarter_less[:], func=SIN, scale=2.0 * math.pi)
+
+
+def tile_attention_pa_kernel(
+    tc, emb, W1_words, W1_scales, W2_words, W2_scales, W3_words, W3_scales, out_0, out_1, out_2
+):
+    nc = tc.nc
+    emb_rows = emb.rearrange("b s e -> (b s) e")
+    weight_words = [W1_words, W2_words, W3_words]
+    weight_scales = [W1_scales, W2_scales, W3_scales]
+    out_rows = [
+        out.rearrange("b h (s c) d -> (b h s) (c d)", c=CHUNKS) for out in (out_0, out_1, out_2)
+    ]
+
+    with ExitStack() as ctx:
+        keep = ctx.enter_context(tc.tile_pool(name="keep", bufs=1))
+        scratch = ctx.enter_context(tc.tile_pool(name="scratch", bufs=1))
+        stage = ctx.enter_context(tc.tile_pool(name="stage", bufs=2))
+        results = ctx.enter_context(tc.tile_pool(name="results", bufs=4))
+        psum_x = ctx.enter_context(tc.psum_pool(name="psum_x", bufs=2))
+        psum_rot = ctx.enter_context(tc.psum_pool(name="psum_rot", bufs=4))
+        psum_plain = ctx.enter_context(tc.psum_pool(name="psum_plain", bufs=2))
+
+        x_sb = keep.tile([P, TOKEN_TILES, FEATURES_IN], BF16)
+        x_words = keep.tile([P, TOKEN_TILES, PASSES * P], U32, align_bytes=64)
+        x_scales = keep.tile([P, TOKEN_TILES, PASSES * P], U8, align_bytes=64)
+        w_words = keep.tile([P, WEIGHTS, PASSES, FEATURES_OUT], U32, align_bytes=64)
+        w_planes = keep.tile([P, 2, FEATURES_OUT], U8, align_bytes=64)
+
+        def load_tokens(m):
+            nc.sync.dma_start(out=x_sb[:, m, :], in_=emb_rows[P * m : P * m + P, :])
+
+        def load_weight(w):
+            first = PACK * ((PASSES * w) % PLANES_PER_TILE)
+            plane_tile = (PASSES * w) // PLANES_PER_TILE
+            for quadrant in range(QUADRANTS):
+                rows = slice(32 * quadrant + first, 32 * quadrant + first + PASSES * 4)
+                nc.sync.dma_start(
+                    out=w_planes[rows, plane_tile, :].bitcast(I32),
+                    in_=weight_scales[w][:, 4 * quadrant : 4 * quadrant + 4, :].bitcast(I32),
+                )
+            for g in range(PASSES):
+                nc.sync.dma_start(
+                    out=w_words[:, w, g, :].bitcast(I32),
+                    in_=weight_words[w][g].rearrange("p n t -> p (n t)").bitcast(I32),
+                )
+
+        nc.vector.memset(w_planes[:].bitcast(I32), 0)
+
+        load_tokens(0)
+        load_weight(0)
+        load_weight(1)
+        load_tokens(1)
+        load_weight(2)
+        for m in range(2, TOKEN_TILES):
+            load_tokens(m)
+
+        cos = keep.tile([P, ROW_PAIRS], F32)
+        sin = keep.tile([P, ROW_PAIRS], F32)
+        neg_sin = keep.tile([P, ROW_PAIRS], F32)
+        build_rotary_tables(nc, scratch, cos, sin, neg_sin)
+
+        identity = keep.tile([P, P], F32)
+        make_identity(nc, identity[:])
+
+        def quantise_tokens(m):
+            pair_words = x_sb[:, m, :].bitcast(F32)
+            flipped = psum_x.tile([P, PASSES, 2, P], F32)
+            for g in range(PASSES):
+                for u in range(2):
+                    nc.tensor.transpose(
+                        flipped[:, g, u, :],
+                        pair_words[:, 256 * g + u : 256 * (g + 1) : 2],
+                        identity[:],
+                    )
+            grouped = stage.tile([P, PASSES * P * PACK], BF16, align_bytes=64)
+            nc.scalar.copy(
+                out=grouped[:].bitcast(F32).rearrange("p (g r u) -> p g r u", g=PASSES, u=2),
+                in_=flipped[:].rearrange("p g u r -> p g r u"),
+            )
+            nc.vector.quantize_mx(
+                out=x_words[:, m, :].bitcast(FP8X4), scales=x_scales[:, m, :], in_=grouped[:]
+            )
+
+        def project(acc, m, w, bank):
+            columns = slice(BANK * bank, BANK * bank + BANK)
+            for g in range(PASSES):
+                plane = PASSES * w + g
+                first = PACK * (plane % PLANES_PER_TILE)
+                nc.tensor.matmul_mx(
+                    out=acc[:],
+                    lhsT=x_words[:, m, P * g : P * g + P].bitcast(FP8X4),
+                    lhsT_scale=x_scales[:, m, P * g : P * g + P],
+                    rhs=w_words[:, w, g, columns].bitcast(FP8X4),
+                    rhs_scale=w_planes[first:P, plane // PLANES_PER_TILE, columns],
+                    start=(g == 0),
+                    stop=(g == PASSES - 1),
+                )
+
+        def rotated_product(m, w):
+            straight = results.tile([P, ROW_PAIRS, 2], F32)
+            crossed = results.tile([P, 2, ROW_PAIRS], F32)
+            for bank in range(BANKS):
+                acc = psum_rot.tile([P, BANK], F32)
+                project(acc, m, w, bank)
+                x_pairs = acc[:].rearrange("p (j e) -> p j e", e=2)
+                pairs = slice(BANK_PAIRS * bank, BANK_PAIRS * bank + BANK_PAIRS)
+                nc.vector.tensor_tensor(
+                    out=straight[:, pairs, :],
+                    in0=x_pairs,
+                    in1=cos[:, pairs].unsqueeze(2).to_broadcast([P, BANK_PAIRS, 2]),
+                    op=ALU.mult,
+                )
+                nc.vector.tensor_tensor(
+                    out=crossed[:, 0, pairs], in0=x_pairs[:, :, 1], in1=neg_sin[:, pairs], op=ALU.mult
+                )
+                nc.vector.tensor_tensor(
+                    out=crossed[:, 1, pairs], in0=x_pairs[:, :, 0], in1=sin[:, pairs], op=ALU.mult
+                )
+            nc.gpsimd.tensor_tensor(
+                out=straight[:],
+                in0=straight[:],
+                in1=crossed[:].rearrange("p e j -> p j e"),
+                op=ALU.add,
+            )
+            nc.sync.dma_start(
+                out=out_rows[w][P * m : P * m + P, :], in_=straight[:].rearrange("p j e -> p (j e)")
+            )
+
+        def plain_product(m, w):
+            plain = results.tile([P, FEATURES_OUT], F32)
+            for bank in range(BANKS):
+                acc = psum_plain.tile([P, BANK], F32)
+                project(acc, m, w, bank)
+                nc.scalar.copy(out=plain[:, BANK * bank : BANK * bank + BANK], in_=acc[:])
+            nc.scalar.dma_start(out=out_rows[w][P * m : P * m + P, :], in_=plain[:])
+
+        quantise_tokens(0)
+        for m in range(TOKEN_TILES + 1):
+            if m + 1 < TOKEN_TILES:
+                quantise_tokens(m + 1)
+            if m < TOKEN_TILES:
+                for w in range(ROTATED):
+                    rotated_product(m, w)
+            if m >= 1:
+                plain_product(m - 1, ROTATED)

@@ -42,7 +42,7 @@ assert 2**DOUBLINGS == PAIRS
 FLOPS = 2 * TOKENS * FEATURES_IN * WEIGHTS * FEATURES_OUT
 
 
-def build_rotary_tables(nc, scratch, cos, sin, neg_sin):
+def build_rotary_tables(nc, scratch, cos, signed_sin):
     position = scratch.tile([P, CHUNKS], F32)
     for half in range(2):
         nc.gpsimd.iota(
@@ -77,8 +77,8 @@ def build_rotary_tables(nc, scratch, cos, sin, neg_sin):
     )
     part = scratch.tile([P, ROW_PAIRS], F32)
     nc.vector.tensor_tensor(out=part[:], in0=turns_flat, in1=whole[:], op=ALU.subtract)
-    nc.scalar.activation(out=sin[:], in_=part[:], func=SIN, scale=2.0 * math.pi)
-    nc.scalar.activation(out=neg_sin[:], in_=part[:], func=SIN, scale=-2.0 * math.pi)
+    nc.scalar.activation(out=signed_sin[:, :, 0], in_=part[:], func=SIN, scale=-2.0 * math.pi)
+    nc.scalar.activation(out=signed_sin[:, :, 1], in_=part[:], func=SIN, scale=2.0 * math.pi)
 
     neg_abs = scratch.tile([P, ROW_PAIRS], F32)
     nc.vector.scalar_tensor_tensor(
@@ -144,9 +144,8 @@ def tile_attention_pa_kernel(
             load_tokens(m)
 
         cos = keep.tile([P, ROW_PAIRS], F32)
-        sin = keep.tile([P, ROW_PAIRS], F32)
-        neg_sin = keep.tile([P, ROW_PAIRS], F32)
-        build_rotary_tables(nc, scratch, cos, sin, neg_sin)
+        signed_sin = keep.tile([P, ROW_PAIRS, 2], F32)
+        build_rotary_tables(nc, scratch, cos, signed_sin)
 
         identity = keep.tile([P, P], F32)
         make_identity(nc, identity[:])
@@ -187,7 +186,7 @@ def tile_attention_pa_kernel(
 
         def rotated_product(m, w):
             straight = results.tile([P, ROW_PAIRS, 2], F32)
-            crossed = results.tile([P, 2, ROW_PAIRS], F32)
+            crossed = results.tile([P, ROW_PAIRS, 2], F32)
             for bank in range(BANKS):
                 acc = psum_rot.tile([P, BANK], F32)
                 project(acc, m, w, bank)
@@ -200,15 +199,15 @@ def tile_attention_pa_kernel(
                     op=ALU.mult,
                 )
                 nc.vector.tensor_tensor(
-                    out=crossed[:, 0, pairs], in0=x_pairs[:, :, 1], in1=neg_sin[:, pairs], op=ALU.mult
-                )
-                nc.vector.tensor_tensor(
-                    out=crossed[:, 1, pairs], in0=x_pairs[:, :, 0], in1=sin[:, pairs], op=ALU.mult
+                    out=crossed[:, pairs, :],
+                    in0=x_pairs[:, :, ::-1],
+                    in1=signed_sin[:, pairs, :],
+                    op=ALU.mult,
                 )
             nc.gpsimd.tensor_tensor(
                 out=straight[:],
                 in0=straight[:],
-                in1=crossed[:].rearrange("p e j -> p j e"),
+                in1=crossed[:],
                 op=ALU.add,
             )
             nc.sync.dma_start(

@@ -31,7 +31,6 @@ BANK_PAIRS = BANK // 2
 ROTATED = 2
 WEIGHTS = 3
 QUADRANTS = 4
-PLANES_PER_TILE = 4
 
 FREQ_RATIO = 10000.0 ** (-2.0 / HEAD_DIM)
 DOUBLINGS = 6
@@ -42,8 +41,7 @@ assert 2**DOUBLINGS == PAIRS
 FLOPS = 2 * TOKENS * FEATURES_IN * WEIGHTS * FEATURES_OUT
 
 
-def build_rotary_tables(nc, scratch, cos, signed_sin):
-    position = scratch.tile([P, CHUNKS], F32)
+def build_positions(nc, position):
     for half in range(2):
         nc.gpsimd.iota(
             position[64 * half : 64 * half + 64, :],
@@ -53,6 +51,8 @@ def build_rotary_tables(nc, scratch, cos, signed_sin):
             allow_small_or_imprecise_dtypes=True,
         )
 
+
+def build_angles(nc, scratch, position, part, neg_abs):
     turns = scratch.tile([P, CHUNKS, PAIRS], F32)
     nc.vector.tensor_scalar_mul(
         out=turns[:, :, 0:1], in0=position[:].unsqueeze(2), scalar1=1.0 / (2.0 * math.pi)
@@ -75,18 +75,18 @@ def build_rotary_tables(nc, scratch, cos, signed_sin):
         op0=ALU.add,
         op1=ALU.subtract,
     )
-    part = scratch.tile([P, ROW_PAIRS], F32)
-    nc.vector.tensor_tensor(out=part[:], in0=turns_flat, in1=whole[:], op=ALU.subtract)
-    nc.scalar.activation(out=signed_sin[:, :, 0], in_=part[:], func=SIN, scale=-2.0 * math.pi)
-    nc.scalar.activation(out=signed_sin[:, :, 1], in_=part[:], func=SIN, scale=2.0 * math.pi)
+    nc.vector.tensor_tensor(out=part[:, 1, :], in0=turns_flat, in1=whole[:], op=ALU.subtract)
+    nc.vector.tensor_tensor(out=part[:, 0, :], in0=whole[:], in1=turns_flat, op=ALU.subtract)
+    nc.vector.tensor_tensor(out=neg_abs[:], in0=part[:, 0, :], in1=part[:, 1, :], op=ALU.min)
 
-    neg_abs = scratch.tile([P, ROW_PAIRS], F32)
-    nc.vector.scalar_tensor_tensor(
-        out=neg_abs[:], in0=part[:], scalar=-1.0, in1=part[:], op0=ALU.mult, op1=ALU.min
+
+def build_sines(nc, part, neg_abs, cos, signed_sin):
+    nc.scalar.activation(
+        out=signed_sin[:], in_=part[:].rearrange("p e j -> p j e"), func=SIN, scale=2.0 * math.pi
     )
-    quarter_less = scratch.tile([P, ROW_PAIRS], F32)
-    nc.vector.tensor_scalar_add(out=quarter_less[:], in0=neg_abs[:], scalar1=0.25)
-    nc.scalar.activation(out=cos[:], in_=quarter_less[:], func=SIN, scale=2.0 * math.pi)
+    nc.scalar.activation(
+        out=cos[:], in_=neg_abs[:], func=SIN, scale=2.0 * math.pi, bias=math.pi / 2.0
+    )
 
 
 def tile_attention_pa_kernel(
@@ -108,50 +108,77 @@ def tile_attention_pa_kernel(
         psum_x = ctx.enter_context(tc.psum_pool(name="psum_x", bufs=2))
         psum_rot = ctx.enter_context(tc.psum_pool(name="psum_rot", bufs=4))
         psum_plain = ctx.enter_context(tc.psum_pool(name="psum_plain", bufs=2))
+        ctx.enter_context(tc.manual_schedule())
 
-        x_sb = keep.tile([P, TOKEN_TILES, FEATURES_IN], BF16)
-        x_words = keep.tile([P, TOKEN_TILES, PASSES * P], U32, align_bytes=64)
-        x_scales = keep.tile([P, TOKEN_TILES, PASSES * P], U8, align_bytes=64)
-        w_words = keep.tile([P, WEIGHTS, PASSES, FEATURES_OUT], U32, align_bytes=64)
-        w_planes = keep.tile([P, 2, FEATURES_OUT], U8, align_bytes=64)
+        x_sb = [keep.tile([P, FEATURES_IN], BF16, name="x_sb%d" % m) for m in range(TOKEN_TILES)]
+        x_words = [
+            keep.tile([P, PASSES * P], U32, align_bytes=64, name="x_words%d" % m)
+            for m in range(TOKEN_TILES)
+        ]
+        x_scales = [
+            keep.tile([P, PASSES * P], U8, align_bytes=64, name="x_scales%d" % m)
+            for m in range(TOKEN_TILES)
+        ]
+        w_words = [
+            [
+                keep.tile([P, PASSES, BANK], U32, align_bytes=64, name="w_words%d_%d" % (w, bank))
+                for bank in range(BANKS)
+            ]
+            for w in range(WEIGHTS)
+        ]
+        w_planes = [
+            keep.tile([P, FEATURES_OUT], U8, align_bytes=64, name="w_planes%d" % w)
+            for w in range(WEIGHTS)
+        ]
 
         def load_tokens(m):
-            nc.sync.dma_start(out=x_sb[:, m, :], in_=emb_rows[P * m : P * m + P, :])
+            nc.sync.dma_start(out=x_sb[m][:], in_=emb_rows[P * m : P * m + P, :])
 
-        def load_weight(w):
-            first = PACK * ((PASSES * w) % PLANES_PER_TILE)
-            plane_tile = (PASSES * w) // PLANES_PER_TILE
+        def load_scales(w):
             for quadrant in range(QUADRANTS):
-                rows = slice(32 * quadrant + first, 32 * quadrant + first + PASSES * 4)
+                rows = slice(32 * quadrant, 32 * quadrant + PASSES * 4)
                 nc.sync.dma_start(
-                    out=w_planes[rows, plane_tile, :].bitcast(I32),
+                    out=w_planes[w][rows, :].bitcast(I32),
                     in_=weight_scales[w][:, 4 * quadrant : 4 * quadrant + 4, :].bitcast(I32),
                 )
-            for g in range(PASSES):
-                nc.sync.dma_start(
-                    out=w_words[:, w, g, :].bitcast(I32),
-                    in_=weight_words[w][g].rearrange("p n t -> p (n t)").bitcast(I32),
-                )
 
-        nc.vector.memset(w_planes[:].bitcast(I32), 0)
+        def load_words(w, bank):
+            nc.sync.dma_start(
+                out=w_words[w][bank][:].bitcast(I32),
+                in_=weight_words[w]
+                .rearrange("g p n t -> p g (n t)")[:, :, PACK * BANK * bank : PACK * BANK * (bank + 1)]
+                .bitcast(I32),
+            )
 
-        load_tokens(0)
-        load_weight(0)
-        load_weight(1)
-        load_tokens(1)
-        load_weight(2)
-        for m in range(2, TOKEN_TILES):
-            load_tokens(m)
+        warm = scratch.tile([P, 2], F32)
+        nc.gpsimd.memset(warm[:, 0:1], 0.0)
+        nc.scalar.activation(out=warm[:, 1:2], in_=warm[:, 0:1], func=SIN)
 
-        cos = keep.tile([P, ROW_PAIRS], F32)
-        signed_sin = keep.tile([P, ROW_PAIRS, 2], F32)
-        build_rotary_tables(nc, scratch, cos, signed_sin)
+        position = scratch.tile([P, CHUNKS], F32)
+        build_positions(nc, position)
 
         identity = keep.tile([P, P], F32)
+        nc.gpsimd.memset(w_planes[0][:].bitcast(F32), 0.0)
         make_identity(nc, identity[:])
+        for w in range(1, WEIGHTS):
+            nc.gpsimd.memset(w_planes[w][:].bitcast(F32), 0.0)
+
+        for w in range(WEIGHTS):
+            load_tokens(w)
+            load_scales(w)
+            for bank in range(BANKS):
+                load_words(w, bank)
+        for m in range(WEIGHTS, TOKEN_TILES):
+            load_tokens(m)
+
+        part = scratch.tile([P, 2, ROW_PAIRS], F32)
+        neg_abs = scratch.tile([P, ROW_PAIRS], F32)
+        cos = keep.tile([P, ROW_PAIRS], F32)
+        signed_sin = keep.tile([P, ROW_PAIRS, 2], F32)
+        build_angles(nc, scratch, position, part, neg_abs)
 
         def quantise_tokens(m):
-            pair_words = x_sb[:, m, :].bitcast(F32)
+            pair_words = x_sb[m][:].bitcast(F32)
             flipped = psum_x.tile([P, PASSES, 2, P], F32)
             for g in range(PASSES):
                 for u in range(2):
@@ -166,20 +193,18 @@ def tile_attention_pa_kernel(
                 in_=flipped[:].rearrange("p g u r -> p g r u"),
             )
             nc.vector.quantize_mx(
-                out=x_words[:, m, :].bitcast(FP8X4), scales=x_scales[:, m, :], in_=grouped[:]
+                out=x_words[m][:].bitcast(FP8X4), scales=x_scales[m][:], in_=grouped[:]
             )
 
         def project(acc, m, w, bank):
             columns = slice(BANK * bank, BANK * bank + BANK)
             for g in range(PASSES):
-                plane = PASSES * w + g
-                first = PACK * (plane % PLANES_PER_TILE)
                 nc.tensor.matmul_mx(
                     out=acc[:],
-                    lhsT=x_words[:, m, P * g : P * g + P].bitcast(FP8X4),
-                    lhsT_scale=x_scales[:, m, P * g : P * g + P],
-                    rhs=w_words[:, w, g, columns].bitcast(FP8X4),
-                    rhs_scale=w_planes[first:P, plane // PLANES_PER_TILE, columns],
+                    lhsT=x_words[m][:, P * g : P * g + P].bitcast(FP8X4),
+                    lhsT_scale=x_scales[m][:, P * g : P * g + P],
+                    rhs=w_words[w][bank][:, g, :].bitcast(FP8X4),
+                    rhs_scale=w_planes[w][4 * g : P, columns],
                     start=(g == 0),
                     stop=(g == PASSES - 1),
                 )
@@ -223,11 +248,13 @@ def tile_attention_pa_kernel(
             nc.scalar.dma_start(out=out_rows[w][P * m : P * m + P, :], in_=plain[:])
 
         quantise_tokens(0)
+        build_sines(nc, part, neg_abs, cos, signed_sin)
         for m in range(TOKEN_TILES + 1):
+            if m < TOKEN_TILES:
+                rotated_product(m, 0)
             if m + 1 < TOKEN_TILES:
                 quantise_tokens(m + 1)
             if m < TOKEN_TILES:
-                for w in range(ROTATED):
-                    rotated_product(m, w)
+                rotated_product(m, 1)
             if m >= 1:
                 plain_product(m - 1, ROTATED)

@@ -36,6 +36,9 @@ FREQ_RATIO = 10000.0 ** (-2.0 / HEAD_DIM)
 DOUBLINGS = 6
 ROUND_TO_WHOLE = 1.5 * 2.0**23
 
+WARM_BEFORE_TOKENS = 4
+WARM_BEFORE_PASSES = 6
+
 assert 2**DOUBLINGS == PAIRS
 
 FLOPS = 2 * TOKENS * FEATURES_IN * WEIGHTS * FEATURES_OUT
@@ -157,6 +160,16 @@ def tile_attention_pa_kernel(
         position = scratch.tile([P, CHUNKS], F32)
         build_positions(nc, position)
 
+        zeros = keep.tile([P, BANK], BF16)
+        nc.vector.memset(zeros[:], 0.0)
+
+        def keep_tensor_busy(matmuls):
+            acc = psum_plain.tile([P, BANK], F32)
+            for i in range(matmuls):
+                nc.tensor.matmul(acc[:], lhsT=zeros[:, 0:P], rhs=zeros[:], start=True, stop=True)
+
+        keep_tensor_busy(WARM_BEFORE_TOKENS)
+
         identity = keep.tile([P, P], F32)
         nc.gpsimd.memset(w_planes[0][:].bitcast(F32), 0.0)
         make_identity(nc, identity[:])
@@ -209,7 +222,7 @@ def tile_attention_pa_kernel(
                     stop=(g == PASSES - 1),
                 )
 
-        def rotated_product(m, w):
+        def rotated_product(m, w, adder):
             straight = results.tile([P, ROW_PAIRS, 2], F32)
             crossed = results.tile([P, ROW_PAIRS, 2], F32)
             for bank in range(BANKS):
@@ -229,12 +242,7 @@ def tile_attention_pa_kernel(
                     in1=signed_sin[:, pairs, :],
                     op=ALU.mult,
                 )
-            nc.gpsimd.tensor_tensor(
-                out=straight[:],
-                in0=straight[:],
-                in1=crossed[:],
-                op=ALU.add,
-            )
+            adder.tensor_tensor(out=straight[:], in0=straight[:], in1=crossed[:], op=ALU.add)
             nc.sync.dma_start(
                 out=out_rows[w][P * m : P * m + P, :], in_=straight[:].rearrange("p j e -> p (j e)")
             )
@@ -248,13 +256,17 @@ def tile_attention_pa_kernel(
             nc.scalar.dma_start(out=out_rows[w][P * m : P * m + P, :], in_=plain[:])
 
         quantise_tokens(0)
+        keep_tensor_busy(WARM_BEFORE_PASSES)
         build_sines(nc, part, neg_abs, cos, signed_sin)
-        for m in range(TOKEN_TILES + 1):
-            if m < TOKEN_TILES:
-                rotated_product(m, 0)
-            if m + 1 < TOKEN_TILES:
+        last = TOKEN_TILES - 1
+        for m in range(TOKEN_TILES):
+            rotated_product(m, 0, nc.gpsimd)
+            if m < last:
                 quantise_tokens(m + 1)
-            if m < TOKEN_TILES:
-                rotated_product(m, 1)
-            if m >= 1:
+                rotated_product(m, 1, nc.gpsimd)
+                if m >= 1:
+                    plain_product(m - 1, ROTATED)
+            else:
                 plain_product(m - 1, ROTATED)
+                plain_product(m, ROTATED)
+                rotated_product(m, 1, nc.vector)

@@ -37,7 +37,6 @@ DOUBLINGS = 6
 ROUND_TO_WHOLE = 1.5 * 2.0**23
 
 WARM_BEFORE_TOKENS = 4
-WARM_BEFORE_PASSES = 6
 
 assert 2**DOUBLINGS == PAIRS
 
@@ -176,13 +175,12 @@ def tile_attention_pa_kernel(
         for w in range(1, WEIGHTS):
             nc.gpsimd.memset(w_planes[w][:].bitcast(F32), 0.0)
 
+        for m in range(TOKEN_TILES):
+            load_tokens(m)
         for w in range(WEIGHTS):
-            load_tokens(w)
             load_scales(w)
             for bank in range(BANKS):
                 load_words(w, bank)
-        for m in range(WEIGHTS, TOKEN_TILES):
-            load_tokens(m)
 
         part = scratch.tile([P, 2, ROW_PAIRS], F32)
         neg_abs = scratch.tile([P, ROW_PAIRS], F32)
@@ -256,13 +254,13 @@ def tile_attention_pa_kernel(
             nc.scalar.dma_start(out=out_rows[w][P * m : P * m + P, :], in_=plain[:])
 
         quantise_tokens(0)
-        keep_tensor_busy(WARM_BEFORE_PASSES)
         build_sines(nc, part, neg_abs, cos, signed_sin)
+        for m in range(1, TOKEN_TILES):
+            quantise_tokens(m)
         last = TOKEN_TILES - 1
         for m in range(TOKEN_TILES):
             rotated_product(m, 0, nc.gpsimd)
             if m < last:
-                quantise_tokens(m + 1)
                 rotated_product(m, 1, nc.gpsimd)
                 if m >= 1:
                     plain_product(m - 1, ROTATED)

@@ -82,10 +82,17 @@ def build_angles(nc, scratch, position, part, neg_abs):
     nc.vector.tensor_tensor(out=neg_abs[:], in0=part[:, 0, :], in1=part[:, 1, :], op=ALU.min)
 
 
-def build_sines(nc, part, neg_abs, cos, signed_sin):
+def build_signed_sines(nc, part, signed_sin, bank):
+    pairs = slice(BANK_PAIRS * bank, BANK_PAIRS * bank + BANK_PAIRS)
     nc.scalar.activation(
-        out=signed_sin[:], in_=part[:].rearrange("p e j -> p j e"), func=SIN, scale=2.0 * math.pi
+        out=signed_sin[:, pairs, :],
+        in_=part[:, :, pairs].rearrange("p e j -> p j e"),
+        func=SIN,
+        scale=2.0 * math.pi,
     )
+
+
+def build_cosines(nc, neg_abs, cos):
     nc.scalar.activation(
         out=cos[:], in_=neg_abs[:], func=SIN, scale=2.0 * math.pi, bias=math.pi / 2.0
     )
@@ -105,11 +112,9 @@ def tile_attention_pa_kernel(
     with ExitStack() as ctx:
         keep = ctx.enter_context(tc.tile_pool(name="keep", bufs=1))
         scratch = ctx.enter_context(tc.tile_pool(name="scratch", bufs=1))
-        stage = ctx.enter_context(tc.tile_pool(name="stage", bufs=2))
+        stage = ctx.enter_context(tc.tile_pool(name="stage", bufs=4))
         results = ctx.enter_context(tc.tile_pool(name="results", bufs=4))
-        psum_x = ctx.enter_context(tc.psum_pool(name="psum_x", bufs=2))
-        psum_rot = ctx.enter_context(tc.psum_pool(name="psum_rot", bufs=4))
-        psum_plain = ctx.enter_context(tc.psum_pool(name="psum_plain", bufs=2))
+        psum = ctx.enter_context(tc.psum_pool(name="psum", bufs=8))
         ctx.enter_context(tc.manual_schedule())
 
         x_sb = [keep.tile([P, FEATURES_IN], BF16, name="x_sb%d" % m) for m in range(TOKEN_TILES)]
@@ -163,7 +168,7 @@ def tile_attention_pa_kernel(
         nc.vector.memset(zeros[:], 0.0)
 
         def keep_tensor_busy(matmuls):
-            acc = psum_plain.tile([P, BANK], F32)
+            acc = psum.tile([P, BANK], F32, tag="bank")
             for i in range(matmuls):
                 nc.tensor.matmul(acc[:], lhsT=zeros[:, 0:P], rhs=zeros[:], start=True, stop=True)
 
@@ -190,7 +195,7 @@ def tile_attention_pa_kernel(
 
         def quantise_tokens(m):
             pair_words = x_sb[m][:].bitcast(F32)
-            flipped = psum_x.tile([P, PASSES, 2, P], F32)
+            flipped = psum.tile([P, PASSES, 2, P], F32, tag="bank")
             for g in range(PASSES):
                 for u in range(2):
                     nc.tensor.transpose(
@@ -224,7 +229,7 @@ def tile_attention_pa_kernel(
             straight = results.tile([P, ROW_PAIRS, 2], F32)
             crossed = results.tile([P, ROW_PAIRS, 2], F32)
             for bank in range(BANKS):
-                acc = psum_rot.tile([P, BANK], F32)
+                acc = psum.tile([P, BANK], F32, tag="bank")
                 project(acc, m, w, bank)
                 x_pairs = acc[:].rearrange("p (j e) -> p j e", e=2)
                 pairs = slice(BANK_PAIRS * bank, BANK_PAIRS * bank + BANK_PAIRS)
@@ -248,15 +253,17 @@ def tile_attention_pa_kernel(
         def plain_product(m, w):
             plain = results.tile([P, FEATURES_OUT], F32)
             for bank in range(BANKS):
-                acc = psum_plain.tile([P, BANK], F32)
+                acc = psum.tile([P, BANK], F32, tag="bank")
                 project(acc, m, w, bank)
                 nc.scalar.copy(out=plain[:, BANK * bank : BANK * bank + BANK], in_=acc[:])
             nc.scalar.dma_start(out=out_rows[w][P * m : P * m + P, :], in_=plain[:])
 
-        quantise_tokens(0)
-        build_sines(nc, part, neg_abs, cos, signed_sin)
-        for m in range(1, TOKEN_TILES):
+        for m in range(TOKEN_TILES):
             quantise_tokens(m)
+            if m == 1 or m == 3:
+                build_signed_sines(nc, part, signed_sin, m // 2)
+            if m == 5:
+                build_cosines(nc, neg_abs, cos)
         last = TOKEN_TILES - 1
         for m in range(TOKEN_TILES):
             rotated_product(m, 0, nc.gpsimd)

@@ -78,7 +78,7 @@ def build_angles(nc, scratch, position, part, neg_abs):
         op1=ALU.subtract,
     )
     nc.vector.tensor_tensor(out=part[:, 1, :], in0=turns_flat, in1=whole[:], op=ALU.subtract)
-    nc.vector.tensor_tensor(out=part[:, 0, :], in0=whole[:], in1=turns_flat, op=ALU.subtract)
+    nc.vector.tensor_scalar_mul(out=part[:, 0, :], in0=part[:, 1, :], scalar1=-1.0)
     nc.vector.tensor_tensor(out=neg_abs[:], in0=part[:, 0, :], in1=part[:, 1, :], op=ALU.min)
 
 
@@ -157,12 +157,11 @@ def tile_attention_pa_kernel(
                 .bitcast(I32),
             )
 
+        position = scratch.tile([P, CHUNKS], F32)
+        build_positions(nc, position)
         warm = scratch.tile([P, 2], F32)
         nc.gpsimd.memset(warm[:, 0:1], 0.0)
         nc.scalar.activation(out=warm[:, 1:2], in_=warm[:, 0:1], func=SIN)
-
-        position = scratch.tile([P, CHUNKS], F32)
-        build_positions(nc, position)
 
         zeros = keep.tile([P, BANK], BF16)
         nc.vector.memset(zeros[:], 0.0)
@@ -225,30 +224,65 @@ def tile_attention_pa_kernel(
                     stop=(g == PASSES - 1),
                 )
 
-        def rotated_product(m, w, adder):
+        def multiply_by_tables(m, w, bank, straight, crossed):
+            acc = psum.tile([P, BANK], F32, tag="bank")
+            project(acc, m, w, bank)
+            x_pairs = acc[:].rearrange("p (j e) -> p j e", e=2)
+            pairs = slice(BANK_PAIRS * bank, BANK_PAIRS * bank + BANK_PAIRS)
+            nc.vector.tensor_tensor(
+                out=straight[:, pairs, :],
+                in0=x_pairs,
+                in1=cos[:, pairs].unsqueeze(2).to_broadcast([P, BANK_PAIRS, 2]),
+                op=ALU.mult,
+            )
+            nc.vector.tensor_tensor(
+                out=crossed[:, pairs, :],
+                in0=x_pairs[:, :, ::-1],
+                in1=signed_sin[:, pairs, :],
+                op=ALU.mult,
+            )
+
+        def add_and_store(engine, m, w, first_bank, banks, straight, crossed):
+            pairs = slice(BANK_PAIRS * first_bank, BANK_PAIRS * (first_bank + banks))
+            engine.tensor_tensor(
+                out=straight[:, pairs, :],
+                in0=straight[:, pairs, :],
+                in1=crossed[:, pairs, :],
+                op=ALU.add,
+            )
+            nc.sync.dma_start(
+                out=out_rows[w][P * m : P * m + P, BANK * first_bank : BANK * (first_bank + banks)],
+                in_=straight[:, pairs, :].rearrange("p j e -> p (j e)"),
+            )
+
+        def rotated_product(m, w):
             straight = results.tile([P, ROW_PAIRS, 2], F32)
             crossed = results.tile([P, ROW_PAIRS, 2], F32)
+            first = m == 0 and w == 0
             for bank in range(BANKS):
-                acc = psum.tile([P, BANK], F32, tag="bank")
-                project(acc, m, w, bank)
-                x_pairs = acc[:].rearrange("p (j e) -> p j e", e=2)
-                pairs = slice(BANK_PAIRS * bank, BANK_PAIRS * bank + BANK_PAIRS)
-                nc.vector.tensor_tensor(
-                    out=straight[:, pairs, :],
-                    in0=x_pairs,
-                    in1=cos[:, pairs].unsqueeze(2).to_broadcast([P, BANK_PAIRS, 2]),
-                    op=ALU.mult,
-                )
-                nc.vector.tensor_tensor(
-                    out=crossed[:, pairs, :],
-                    in0=x_pairs[:, :, ::-1],
-                    in1=signed_sin[:, pairs, :],
-                    op=ALU.mult,
-                )
-            adder.tensor_tensor(out=straight[:], in0=straight[:], in1=crossed[:], op=ALU.add)
-            nc.sync.dma_start(
-                out=out_rows[w][P * m : P * m + P, :], in_=straight[:].rearrange("p j e -> p (j e)")
-            )
+                multiply_by_tables(m, w, bank, straight, crossed)
+                if first:
+                    add_and_store(nc.gpsimd, m, w, bank, 1, straight, crossed)
+            if not first:
+                add_and_store(nc.gpsimd, m, w, 0, BANKS, straight, crossed)
+
+        def last_rotated_products(m):
+            terms = {}
+            for w in range(ROTATED):
+                straight = results.tile([P, ROW_PAIRS, 2], F32)
+                crossed = results.tile([P, ROW_PAIRS, 2], F32)
+                terms[w] = (straight, crossed)
+                for bank in range(BANKS):
+                    multiply_by_tables(m, w, bank, straight, crossed)
+                    if w == 0 and bank == 0:
+                        add_and_store(nc.gpsimd, m, w, bank, 1, straight, crossed)
+                if w == 0:
+                    plain_product(m - 1, ROTATED)
+                    plain_product(m, ROTATED)
+            for w in range(ROTATED):
+                for bank in range(BANKS):
+                    if w > 0 or bank > 0:
+                        add_and_store(nc.vector, m, w, bank, 1, terms[w][0], terms[w][1])
 
         def plain_product(m, w):
             plain = results.tile([P, FEATURES_OUT], F32)
@@ -260,18 +294,13 @@ def tile_attention_pa_kernel(
 
         for m in range(TOKEN_TILES):
             quantise_tokens(m)
-            if m == 1 or m == 3:
-                build_signed_sines(nc, part, signed_sin, m // 2)
-            if m == 5:
-                build_cosines(nc, neg_abs, cos)
+        build_cosines(nc, neg_abs, cos)
+        for bank in range(BANKS):
+            build_signed_sines(nc, part, signed_sin, bank)
         last = TOKEN_TILES - 1
-        for m in range(TOKEN_TILES):
-            rotated_product(m, 0, nc.gpsimd)
-            if m < last:
-                rotated_product(m, 1, nc.gpsimd)
-                if m >= 1:
-                    plain_product(m - 1, ROTATED)
-            else:
+        for m in range(last):
+            rotated_product(m, 0)
+            rotated_product(m, 1)
+            if m >= 1:
                 plain_product(m - 1, ROTATED)
-                plain_product(m, ROTATED)
-                rotated_product(m, 1, nc.vector)
+        last_rotated_products(last)

@@ -113,7 +113,7 @@ def tile_attention_pa_kernel(
         keep = ctx.enter_context(tc.tile_pool(name="keep", bufs=1))
         scratch = ctx.enter_context(tc.tile_pool(name="scratch", bufs=1))
         stage = ctx.enter_context(tc.tile_pool(name="stage", bufs=4))
-        results = ctx.enter_context(tc.tile_pool(name="results", bufs=4))
+        results = ctx.enter_context(tc.tile_pool(name="results", bufs=8))
         psum = ctx.enter_context(tc.psum_pool(name="psum", bufs=8))
         ctx.enter_context(tc.manual_schedule())
 

@@ -33,12 +33,13 @@ WEIGHTS = 3
 QUADRANTS = 4
 
 FREQ_RATIO = 10000.0 ** (-2.0 / HEAD_DIM)
-DOUBLINGS = 6
+FINE = 8
+COARSE = PAIRS // FINE
 ROUND_TO_WHOLE = 1.5 * 2.0**23
 
-WARM_BEFORE_TOKENS = 4
+VECTOR_COPIES = (3, 6)
 
-assert 2**DOUBLINGS == PAIRS
+WARM_BEFORE_TOKENS = 4
 
 FLOPS = 2 * TOKENS * FEATURES_IN * WEIGHTS * FEATURES_OUT
 
@@ -54,47 +55,80 @@ def build_positions(nc, position):
         )
 
 
-def build_angles(nc, scratch, position, part, neg_abs):
-    turns = scratch.tile([P, CHUNKS, PAIRS], F32)
-    nc.vector.tensor_scalar_mul(
-        out=turns[:, :, 0:1], in0=position[:].unsqueeze(2), scalar1=1.0 / (2.0 * math.pi)
-    )
-    for step in range(DOUBLINGS):
-        width = 2**step
+def build_angles(nc, scratch, position, part, shifted):
+    one = scratch.tile([P, 1], F32)
+    nc.vector.memset(one[:], 1.0)
+    fine = scratch.tile([P, FINE], F32)
+    coarse = scratch.tile([P, COARSE], F32)
+    for b in range(FINE):
         nc.vector.tensor_scalar_mul(
-            out=turns[:, :, width : 2 * width],
-            in0=turns[:, :, 0:width],
-            scalar1=FREQ_RATIO**width,
+            out=fine[:, b : b + 1], in0=one[:], scalar1=FREQ_RATIO**b / (2.0 * math.pi)
         )
-    turns_flat = turns[:].rearrange("p c i -> p (c i)")
-
-    whole = scratch.tile([P, ROW_PAIRS], F32)
-    nc.vector.tensor_scalar(
-        out=whole[:],
-        in0=turns_flat,
-        scalar1=ROUND_TO_WHOLE,
-        scalar2=ROUND_TO_WHOLE,
-        op0=ALU.add,
-        op1=ALU.subtract,
+    for a in range(COARSE):
+        nc.vector.tensor_scalar_mul(
+            out=coarse[:, a : a + 1], in0=one[:], scalar1=FREQ_RATIO ** (FINE * a)
+        )
+    scaled = scratch.tile([P, CHUNKS, COARSE], F32)
+    nc.vector.tensor_tensor(
+        out=scaled[:],
+        in0=position[:].unsqueeze(2).to_broadcast([P, CHUNKS, COARSE]),
+        in1=coarse[:].unsqueeze(1).to_broadcast([P, CHUNKS, COARSE]),
+        op=ALU.mult,
     )
-    nc.vector.tensor_tensor(out=part[:, 1, :], in0=turns_flat, in1=whole[:], op=ALU.subtract)
-    nc.vector.tensor_scalar_mul(out=part[:, 0, :], in0=part[:, 1, :], scalar1=-1.0)
-    nc.vector.tensor_tensor(out=neg_abs[:], in0=part[:, 0, :], in1=part[:, 1, :], op=ALU.min)
+    scaled_flat = scaled[:].rearrange("p c a -> p (c a)")
+    turns = scratch.tile([P, CHUNKS * COARSE, FINE], F32)
+    turns_flat = turns[:].rearrange("p r b -> p (r b)")
+    whole = scratch.tile([P, ROW_PAIRS], F32)
+    rows = CHUNKS * COARSE // BANKS
+    banks = [slice(BANK_PAIRS * bank, BANK_PAIRS * (bank + 1)) for bank in range(BANKS)]
+    for bank in range(BANKS):
+        nc.vector.tensor_tensor(
+            out=turns[:, rows * bank : rows * (bank + 1), :],
+            in0=scaled_flat[:, rows * bank : rows * (bank + 1)]
+            .unsqueeze(2)
+            .to_broadcast([P, rows, FINE]),
+            in1=fine[:].unsqueeze(1).to_broadcast([P, rows, FINE]),
+            op=ALU.mult,
+        )
+    for pairs in banks:
+        nc.vector.tensor_scalar(
+            out=whole[:, pairs],
+            in0=turns_flat[:, pairs],
+            scalar1=ROUND_TO_WHOLE,
+            scalar2=ROUND_TO_WHOLE,
+            op0=ALU.add,
+            op1=ALU.subtract,
+        )
+    for pairs in banks:
+        nc.vector.tensor_tensor(
+            out=part[:, pairs], in0=turns_flat[:, pairs], in1=whole[:, pairs], op=ALU.subtract
+        )
+    for pairs in banks:
+        nc.vector.scalar_tensor_tensor(
+            out=shifted[:, pairs],
+            in0=part[:, pairs],
+            scalar=0.25,
+            in1=part[:, pairs],
+            op0=ALU.is_gt,
+            op1=ALU.subtract,
+        )
 
 
-def build_signed_sines(nc, part, signed_sin, bank):
+def build_sines(nc, part, signed_sin, bank):
+    pairs = slice(BANK_PAIRS * bank, BANK_PAIRS * bank + BANK_PAIRS)
+    for sign in range(2):
+        nc.scalar.activation(
+            out=signed_sin[:, sign, pairs],
+            in_=part[:, pairs],
+            func=SIN,
+            scale=(2 * sign - 1) * 2.0 * math.pi,
+        )
+
+
+def build_cosines(nc, shifted, cos, bank):
     pairs = slice(BANK_PAIRS * bank, BANK_PAIRS * bank + BANK_PAIRS)
     nc.scalar.activation(
-        out=signed_sin[:, pairs, :],
-        in_=part[:, :, pairs].rearrange("p e j -> p j e"),
-        func=SIN,
-        scale=2.0 * math.pi,
-    )
-
-
-def build_cosines(nc, neg_abs, cos):
-    nc.scalar.activation(
-        out=cos[:], in_=neg_abs[:], func=SIN, scale=2.0 * math.pi, bias=math.pi / 2.0
+        out=cos[:, pairs], in_=shifted[:, pairs], func=SIN, scale=-2.0 * math.pi, bias=math.pi / 2.0
     )
 
 
@@ -112,7 +146,7 @@ def tile_attention_pa_kernel(
     with ExitStack() as ctx:
         keep = ctx.enter_context(tc.tile_pool(name="keep", bufs=1))
         scratch = ctx.enter_context(tc.tile_pool(name="scratch", bufs=1))
-        stage = ctx.enter_context(tc.tile_pool(name="stage", bufs=4))
+        stage = ctx.enter_context(tc.tile_pool(name="stage", bufs=8))
         results = ctx.enter_context(tc.tile_pool(name="results", bufs=8))
         psum = ctx.enter_context(tc.psum_pool(name="psum", bufs=8))
         ctx.enter_context(tc.manual_schedule())
@@ -174,9 +208,8 @@ def tile_attention_pa_kernel(
         keep_tensor_busy(WARM_BEFORE_TOKENS)
 
         identity = keep.tile([P, P], F32)
-        nc.gpsimd.memset(w_planes[0][:].bitcast(F32), 0.0)
         make_identity(nc, identity[:])
-        for w in range(1, WEIGHTS):
+        for w in range(WEIGHTS):
             nc.gpsimd.memset(w_planes[w][:].bitcast(F32), 0.0)
 
         for m in range(TOKEN_TILES):
@@ -186,13 +219,15 @@ def tile_attention_pa_kernel(
             for bank in range(BANKS):
                 load_words(w, bank)
 
-        part = scratch.tile([P, 2, ROW_PAIRS], F32)
-        neg_abs = scratch.tile([P, ROW_PAIRS], F32)
+        part = scratch.tile([P, ROW_PAIRS], F32)
+        shifted = scratch.tile([P, ROW_PAIRS], F32)
         cos = keep.tile([P, ROW_PAIRS], F32)
-        signed_sin = keep.tile([P, ROW_PAIRS, 2], F32)
-        build_angles(nc, scratch, position, part, neg_abs)
+        signed_sin = keep.tile([P, 2, ROW_PAIRS], F32)
+        build_angles(nc, scratch, position, part, shifted)
 
-        def quantise_tokens(m):
+        grouped = {}
+
+        def turn_tokens(m):
             pair_words = x_sb[m][:].bitcast(F32)
             flipped = psum.tile([P, PASSES, 2, P], F32, tag="bank")
             for g in range(PASSES):
@@ -202,13 +237,17 @@ def tile_attention_pa_kernel(
                         pair_words[:, 256 * g + u : 256 * (g + 1) : 2],
                         identity[:],
                     )
-            grouped = stage.tile([P, PASSES * P * PACK], BF16, align_bytes=64)
-            nc.scalar.copy(
-                out=grouped[:].bitcast(F32).rearrange("p (g r u) -> p g r u", g=PASSES, u=2),
-                in_=flipped[:].rearrange("p g u r -> p g r u"),
-            )
+            grouped[m] = stage.tile([P, PASSES * P * PACK], BF16, align_bytes=64, name="grouped")
+            source = flipped[:].rearrange("p g u r -> p g r u")
+            target = grouped[m][:].bitcast(F32).rearrange("p (g r u) -> p g r u", g=PASSES, u=2)
+            if m in VECTOR_COPIES:
+                nc.vector.tensor_copy(out=target, in_=source)
+            else:
+                nc.scalar.copy(out=target, in_=source)
+
+        def quantise_tokens(m):
             nc.vector.quantize_mx(
-                out=x_words[m][:].bitcast(FP8X4), scales=x_scales[m][:], in_=grouped[:]
+                out=x_words[m][:].bitcast(FP8X4), scales=x_scales[m][:], in_=grouped[m][:]
             )
 
         def project(acc, m, w, bank):
@@ -238,7 +277,7 @@ def tile_attention_pa_kernel(
             nc.vector.tensor_tensor(
                 out=crossed[:, pairs, :],
                 in0=x_pairs[:, :, ::-1],
-                in1=signed_sin[:, pairs, :],
+                in1=signed_sin[:, :, pairs].rearrange("p e j -> p j e"),
                 op=ALU.mult,
             )
 
@@ -293,10 +332,16 @@ def tile_attention_pa_kernel(
             nc.scalar.dma_start(out=out_rows[w][P * m : P * m + P, :], in_=plain[:])
 
         for m in range(TOKEN_TILES):
-            quantise_tokens(m)
-        build_cosines(nc, neg_abs, cos)
-        for bank in range(BANKS):
-            build_signed_sines(nc, part, signed_sin, bank)
+            turn_tokens(m)
+            if m == 0:
+                build_sines(nc, part, signed_sin, 0)
+            elif m == 1:
+                build_cosines(nc, shifted, cos, 0)
+            if m > 0:
+                quantise_tokens(m - 1)
+        quantise_tokens(TOKEN_TILES - 1)
+        build_cosines(nc, shifted, cos, 1)
+        build_sines(nc, part, signed_sin, 1)
         last = TOKEN_TILES - 1
         for m in range(last):
             rotated_product(m, 0)

@@ -37,9 +37,8 @@ FINE = 8
 COARSE = PAIRS // FINE
 ROUND_TO_WHOLE = 1.5 * 2.0**23
 
-VECTOR_COPIES = (3, 6)
-
-WARM_BEFORE_TOKENS = 4
+TENSOR_ADDS = (2, 4)
+VECTOR_COPIES = (0, 4)
 
 FLOPS = 2 * TOKENS * FEATURES_IN * WEIGHTS * FEATURES_OUT
 
@@ -59,22 +58,17 @@ def build_angles(nc, scratch, position, part, shifted):
     one = scratch.tile([P, 1], F32)
     nc.vector.memset(one[:], 1.0)
     fine = scratch.tile([P, FINE], F32)
-    coarse = scratch.tile([P, COARSE], F32)
+    scaled = scratch.tile([P, CHUNKS, COARSE], F32)
     for b in range(FINE):
         nc.vector.tensor_scalar_mul(
             out=fine[:, b : b + 1], in0=one[:], scalar1=FREQ_RATIO**b / (2.0 * math.pi)
         )
     for a in range(COARSE):
         nc.vector.tensor_scalar_mul(
-            out=coarse[:, a : a + 1], in0=one[:], scalar1=FREQ_RATIO ** (FINE * a)
+            out=scaled[:, :, a : a + 1],
+            in0=position[:].unsqueeze(2),
+            scalar1=FREQ_RATIO ** (FINE * a),
         )
-    scaled = scratch.tile([P, CHUNKS, COARSE], F32)
-    nc.vector.tensor_tensor(
-        out=scaled[:],
-        in0=position[:].unsqueeze(2).to_broadcast([P, CHUNKS, COARSE]),
-        in1=coarse[:].unsqueeze(1).to_broadcast([P, CHUNKS, COARSE]),
-        op=ALU.mult,
-    )
     scaled_flat = scaled[:].rearrange("p c a -> p (c a)")
     turns = scratch.tile([P, CHUNKS * COARSE, FINE], F32)
     turns_flat = turns[:].rearrange("p r b -> p (r b)")
@@ -197,16 +191,6 @@ def tile_attention_pa_kernel(
         nc.gpsimd.memset(warm[:, 0:1], 0.0)
         nc.scalar.activation(out=warm[:, 1:2], in_=warm[:, 0:1], func=SIN)
 
-        zeros = keep.tile([P, BANK], BF16)
-        nc.vector.memset(zeros[:], 0.0)
-
-        def keep_tensor_busy(matmuls):
-            acc = psum.tile([P, BANK], F32, tag="bank")
-            for i in range(matmuls):
-                nc.tensor.matmul(acc[:], lhsT=zeros[:, 0:P], rhs=zeros[:], start=True, stop=True)
-
-        keep_tensor_busy(WARM_BEFORE_TOKENS)
-
         identity = keep.tile([P, P], F32)
         make_identity(nc, identity[:])
         for w in range(WEIGHTS):
@@ -294,34 +278,50 @@ def tile_attention_pa_kernel(
                 in_=straight[:, pairs, :].rearrange("p j e -> p (j e)"),
             )
 
-        def rotated_product(m, w):
-            straight = results.tile([P, ROW_PAIRS, 2], F32)
-            crossed = results.tile([P, ROW_PAIRS, 2], F32)
-            first = m == 0 and w == 0
+        def new_terms():
+            straight = results.tile([P, ROW_PAIRS, 2], F32, name="straight")
+            crossed = results.tile([P, ROW_PAIRS, 2], F32, name="crossed")
+            return straight, crossed
+
+        def rotated_bank(m, w, bank, terms):
+            multiply_by_tables(m, w, bank, *terms)
+            add_and_store(nc.gpsimd, m, w, bank, 1, *terms)
+
+        def rotated_product(m, w, gpsimd_banks):
+            terms = new_terms()
             for bank in range(BANKS):
-                multiply_by_tables(m, w, bank, straight, crossed)
-                if first:
-                    add_and_store(nc.gpsimd, m, w, bank, 1, straight, crossed)
-            if not first:
-                add_and_store(nc.gpsimd, m, w, 0, BANKS, straight, crossed)
+                multiply_by_tables(m, w, bank, *terms)
+            add_and_store(nc.gpsimd, m, w, 0, gpsimd_banks, *terms)
+            return terms
+
+        def tensor_add_and_store(m, w, bank, terms):
+            columns = slice(BANK * bank, BANK * bank + BANK)
+            acc = psum.tile([P, BANK], F32, tag="bank")
+            for i in range(len(terms)):
+                nc.tensor.matmul(
+                    acc[:],
+                    lhsT=identity[:],
+                    rhs=terms[i][:].rearrange("p j e -> p (j e)")[:, columns],
+                    start=(i == 0),
+                    stop=(i == len(terms) - 1),
+                )
+            summed = results.tile([P, BANK], F32)
+            nc.scalar.copy(out=summed[:], in_=acc[:])
+            nc.scalar.dma_start(out=out_rows[w][P * m : P * m + P, columns], in_=summed[:])
 
         def last_rotated_products(m):
             terms = {}
             for w in range(ROTATED):
-                straight = results.tile([P, ROW_PAIRS, 2], F32)
-                crossed = results.tile([P, ROW_PAIRS, 2], F32)
-                terms[w] = (straight, crossed)
-                for bank in range(BANKS):
-                    multiply_by_tables(m, w, bank, straight, crossed)
-                    if w == 0 and bank == 0:
-                        add_and_store(nc.gpsimd, m, w, bank, 1, straight, crossed)
+                terms[w] = new_terms()
+                rotated_bank(m, w, 0, terms[w])
+                multiply_by_tables(m, w, 1, *terms[w])
                 if w == 0:
                     plain_product(m - 1, ROTATED)
                     plain_product(m, ROTATED)
-            for w in range(ROTATED):
-                for bank in range(BANKS):
-                    if w > 0 or bank > 0:
-                        add_and_store(nc.vector, m, w, bank, 1, terms[w][0], terms[w][1])
+            if m - 1 in TENSOR_ADDS:
+                tensor_add_and_store(m - 1, 1, 1, waiting[m - 1])
+            tensor_add_and_store(m, 0, 1, terms[0])
+            add_and_store(nc.vector, m, 1, 1, 1, *terms[1])
 
         def plain_product(m, w):
             plain = results.tile([P, FEATURES_OUT], F32)
@@ -331,21 +331,33 @@ def tile_attention_pa_kernel(
                 nc.scalar.copy(out=plain[:, BANK * bank : BANK * bank + BANK], in_=acc[:])
             nc.scalar.dma_start(out=out_rows[w][P * m : P * m + P, :], in_=plain[:])
 
+        build_sines(nc, part, signed_sin, 0)
         for m in range(TOKEN_TILES):
             turn_tokens(m)
             if m == 0:
-                build_sines(nc, part, signed_sin, 0)
-            elif m == 1:
                 build_cosines(nc, shifted, cos, 0)
             if m > 0:
                 quantise_tokens(m - 1)
         quantise_tokens(TOKEN_TILES - 1)
         build_cosines(nc, shifted, cos, 1)
         build_sines(nc, part, signed_sin, 1)
+        first_terms = [new_terms() for m in range(2)]
+        rotated_bank(0, 0, 0, first_terms[0])
+        rotated_bank(1, 0, 0, first_terms[1])
+        rotated_bank(0, 0, 1, first_terms[0])
+        rotated_product(0, 1, BANKS)
+        rotated_bank(1, 0, 1, first_terms[1])
+        rotated_product(1, 1, BANKS)
+        plain_product(0, ROTATED)
+        waiting = {}
         last = TOKEN_TILES - 1
-        for m in range(last):
-            rotated_product(m, 0)
-            rotated_product(m, 1)
-            if m >= 1:
-                plain_product(m - 1, ROTATED)
+        for m in range(2, last):
+            rotated_product(m, 0, BANKS)
+            if m in TENSOR_ADDS:
+                waiting[m] = rotated_product(m, 1, 1)
+            else:
+                rotated_product(m, 1, BANKS)
+            if m - 1 in TENSOR_ADDS:
+                tensor_add_and_store(m - 1, 1, 1, waiting[m - 1])
+            plain_product(m - 1, ROTATED)
         last_rotated_products(last)

@@ -37,8 +37,8 @@ FINE = 8
 COARSE = PAIRS // FINE
 ROUND_TO_WHOLE = 1.5 * 2.0**23
 
-TENSOR_ADDS = (2, 4)
-VECTOR_COPIES = (0, 4)
+TENSOR_ADDS = (2, 4, 6)
+VECTOR_COPIES = (0, 3, 5)
 
 FLOPS = 2 * TOKENS * FEATURES_IN * WEIGHTS * FEATURES_OUT
 
@@ -156,7 +156,10 @@ def tile_attention_pa_kernel(
         ]
         w_words = [
             [
-                keep.tile([P, PASSES, BANK], U32, align_bytes=64, name="w_words%d_%d" % (w, bank))
+                [
+                    keep.tile([P, BANK], U32, align_bytes=64, name="w_words%d_%d_%d" % (w, bank, g))
+                    for g in range(PASSES)
+                ]
                 for bank in range(BANKS)
             ]
             for w in range(WEIGHTS)
@@ -178,12 +181,13 @@ def tile_attention_pa_kernel(
                 )
 
         def load_words(w, bank):
-            nc.sync.dma_start(
-                out=w_words[w][bank][:].bitcast(I32),
-                in_=weight_words[w]
-                .rearrange("g p n t -> p g (n t)")[:, :, PACK * BANK * bank : PACK * BANK * (bank + 1)]
-                .bitcast(I32),
-            )
+            for g in range(PASSES):
+                nc.sync.dma_start(
+                    out=w_words[w][bank][g][:].bitcast(I32),
+                    in_=weight_words[w][g]
+                    .rearrange("p n t -> p (n t)")[:, PACK * BANK * bank : PACK * BANK * (bank + 1)]
+                    .bitcast(I32),
+                )
 
         position = scratch.tile([P, CHUNKS], F32)
         build_positions(nc, position)
@@ -241,7 +245,7 @@ def tile_attention_pa_kernel(
                     out=acc[:],
                     lhsT=x_words[m][:, P * g : P * g + P].bitcast(FP8X4),
                     lhsT_scale=x_scales[m][:, P * g : P * g + P],
-                    rhs=w_words[w][bank][:, g, :].bitcast(FP8X4),
+                    rhs=w_words[w][bank][g][:].bitcast(FP8X4),
                     rhs_scale=w_planes[w][4 * g : P, columns],
                     start=(g == 0),
                     stop=(g == PASSES - 1),
@@ -265,8 +269,8 @@ def tile_attention_pa_kernel(
                 op=ALU.mult,
             )
 
-        def add_and_store(engine, m, w, first_bank, banks, straight, crossed):
-            pairs = slice(BANK_PAIRS * first_bank, BANK_PAIRS * (first_bank + banks))
+        def add_and_store(engine, m, w, start, width, straight, crossed):
+            pairs = slice(start // 2, (start + width) // 2)
             engine.tensor_tensor(
                 out=straight[:, pairs, :],
                 in0=straight[:, pairs, :],
@@ -274,7 +278,7 @@ def tile_attention_pa_kernel(
                 op=ALU.add,
             )
             nc.sync.dma_start(
-                out=out_rows[w][P * m : P * m + P, BANK * first_bank : BANK * (first_bank + banks)],
+                out=out_rows[w][P * m : P * m + P, start : start + width],
                 in_=straight[:, pairs, :].rearrange("p j e -> p (j e)"),
             )
 
@@ -285,13 +289,13 @@ def tile_attention_pa_kernel(
 
         def rotated_bank(m, w, bank, terms):
             multiply_by_tables(m, w, bank, *terms)
-            add_and_store(nc.gpsimd, m, w, bank, 1, *terms)
+            add_and_store(nc.gpsimd, m, w, BANK * bank, BANK, *terms)
 
         def rotated_product(m, w, gpsimd_banks):
             terms = new_terms()
             for bank in range(BANKS):
                 multiply_by_tables(m, w, bank, *terms)
-            add_and_store(nc.gpsimd, m, w, 0, gpsimd_banks, *terms)
+            add_and_store(nc.gpsimd, m, w, 0, BANK * gpsimd_banks, *terms)
             return terms
 
         def tensor_add_and_store(m, w, bank, terms):
@@ -318,10 +322,11 @@ def tile_attention_pa_kernel(
                 if w == 0:
                     plain_product(m - 1, ROTATED)
                     plain_product(m, ROTATED)
-            if m - 1 in TENSOR_ADDS:
-                tensor_add_and_store(m - 1, 1, 1, waiting[m - 1])
-            tensor_add_and_store(m, 0, 1, terms[0])
-            add_and_store(nc.vector, m, 1, 1, 1, *terms[1])
+            tensor_add_and_store(m - 1, 1, 1, waiting[m - 1])
+            add_and_store(nc.vector, m, 0, BANK, BANK, *terms[0])
+            half = BANK // 2
+            for i in range(2):
+                add_and_store(nc.vector, m, 1, BANK + half * i, half, *terms[1])
 
         def plain_product(m, w):
             plain = results.tile([P, FEATURES_OUT], F32)
@@ -353,11 +358,11 @@ def tile_attention_pa_kernel(
         last = TOKEN_TILES - 1
         for m in range(2, last):
             rotated_product(m, 0, BANKS)
+            plain_product(m - 1, ROTATED)
             if m in TENSOR_ADDS:
                 waiting[m] = rotated_product(m, 1, 1)
             else:
                 rotated_product(m, 1, BANKS)
             if m - 1 in TENSOR_ADDS:
                 tensor_add_and_store(m - 1, 1, 1, waiting[m - 1])
-            plain_product(m - 1, ROTATED)
         last_rotated_products(last)

@@ -215,23 +215,32 @@ def tile_attention_pa_kernel(
 
         grouped = {}
 
+        def copies_of(m):
+            if m == TOKEN_TILES - 1:
+                return (((0,), nc.scalar.copy), ((1,), nc.vector.tensor_copy))
+            if m in VECTOR_COPIES:
+                return (((0, 1), nc.vector.tensor_copy),)
+            return (((0, 1), nc.scalar.copy),)
+
         def turn_tokens(m):
             pair_words = x_sb[m][:].bitcast(F32)
-            flipped = psum.tile([P, PASSES, 2, P], F32, tag="bank")
-            for g in range(PASSES):
-                for u in range(2):
-                    nc.tensor.transpose(
-                        flipped[:, g, u, :],
-                        pair_words[:, 256 * g + u : 256 * (g + 1) : 2],
-                        identity[:],
-                    )
             grouped[m] = stage.tile([P, PASSES * P * PACK], BF16, align_bytes=64, name="grouped")
-            source = flipped[:].rearrange("p g u r -> p g r u")
-            target = grouped[m][:].bitcast(F32).rearrange("p (g r u) -> p g r u", g=PASSES, u=2)
-            if m in VECTOR_COPIES:
-                nc.vector.tensor_copy(out=target, in_=source)
-            else:
-                nc.scalar.copy(out=target, in_=source)
+            for passes, engine_copy in copies_of(m):
+                flipped = psum.tile([P, len(passes), 2, P], F32, tag="bank")
+                for i in range(len(passes)):
+                    for u in range(2):
+                        nc.tensor.transpose(
+                            flipped[:, i, u, :],
+                            pair_words[:, 256 * passes[i] + u : 256 * (passes[i] + 1) : 2],
+                            identity[:],
+                        )
+                words = slice(2 * P * passes[0], 2 * P * (passes[-1] + 1))
+                engine_copy(
+                    out=grouped[m][:]
+                    .bitcast(F32)[:, words]
+                    .rearrange("p (g r u) -> p g r u", g=len(passes), u=2),
+                    in_=flipped[:].rearrange("p g u r -> p g r u"),
+                )
 
         def quantise_tokens(m):
             nc.vector.quantize_mx(

@@ -323,19 +323,17 @@ def tile_attention_pa_kernel(
             nc.scalar.dma_start(out=out_rows[w][P * m : P * m + P, columns], in_=summed[:])
 
         def last_rotated_products(m):
-            terms = {}
-            for w in range(ROTATED):
-                terms[w] = new_terms()
-                rotated_bank(m, w, 0, terms[w])
-                multiply_by_tables(m, w, 1, *terms[w])
-                if w == 0:
-                    plain_product(m - 1, ROTATED)
-                    plain_product(m, ROTATED)
+            terms = new_terms()
+            for bank in range(BANKS):
+                rotated_bank(m, 0, bank, terms)
+            plain_product(m - 1, ROTATED)
+            plain_product(m, ROTATED)
+            terms = new_terms()
+            for bank in range(BANKS):
+                multiply_by_tables(m, 1, bank, *terms)
             tensor_add_and_store(m - 1, 1, 1, waiting[m - 1])
-            add_and_store(nc.vector, m, 0, BANK, BANK, *terms[0])
-            half = BANK // 2
-            for i in range(2):
-                add_and_store(nc.vector, m, 1, BANK + half * i, half, *terms[1])
+            for start, width in ((0, BANK), (BANK, BANK // 2), (BANK + BANK // 2, BANK // 2)):
+                add_and_store(nc.vector, m, 1, start, width, *terms)
 
         def plain_product(m, w):
             plain = results.tile([P, FEATURES_OUT], F32)

import math
from contextlib import ExitStack

import concourse.mybir as mybir
from concourse.masks import make_identity

F32 = mybir.dt.float32
BF16 = mybir.dt.bfloat16
I32 = mybir.dt.int32
U32 = mybir.dt.uint32
U8 = mybir.dt.uint8
FP8X4 = mybir.dt.float8_e4m3fn_x4
ALU = mybir.AluOpType
SIN = mybir.ActivationFunctionType.Sin

P = 128
PACK = 4
K_PASS = P * PACK
TOKENS = 1024
FEATURES_IN = 1024
FEATURES_OUT = 1024
PASSES = FEATURES_IN // K_PASS
TOKEN_TILES = TOKENS // P
BANK = 512
BANKS = FEATURES_OUT // BANK
HEAD_DIM = 128
CHUNKS = FEATURES_OUT // HEAD_DIM
PAIRS = HEAD_DIM // 2
ROW_PAIRS = FEATURES_OUT // 2
BANK_PAIRS = BANK // 2
ROTATED = 2
WEIGHTS = 3
QUADRANTS = 4

FREQ_RATIO = 10000.0 ** (-2.0 / HEAD_DIM)
FINE = 8
COARSE = PAIRS // FINE
ROUND_TO_WHOLE = 1.5 * 2.0**23

TENSOR_ADDS = (2, 4, 6)
VECTOR_COPIES = (0, 3, 5)

FLOPS = 2 * TOKENS * FEATURES_IN * WEIGHTS * FEATURES_OUT


def build_positions(nc, position):
    for half in range(2):
        nc.gpsimd.iota(
            position[64 * half : 64 * half + 64, :],
            pattern=[[1, CHUNKS]],
            base=0,
            channel_multiplier=CHUNKS,
            allow_small_or_imprecise_dtypes=True,
        )


def build_angles(nc, scratch, position, part, shifted):
    one = scratch.tile([P, 1], F32)
    nc.vector.memset(one[:], 1.0)
    fine = scratch.tile([P, FINE], F32)
    scaled = scratch.tile([P, CHUNKS, COARSE], F32)
    for b in range(FINE):
        nc.vector.tensor_scalar_mul(
            out=fine[:, b : b + 1], in0=one[:], scalar1=FREQ_RATIO**b / (2.0 * math.pi)
        )
    for a in range(COARSE):
        nc.vector.tensor_scalar_mul(
            out=scaled[:, :, a : a + 1],
            in0=position[:].unsqueeze(2),
            scalar1=FREQ_RATIO ** (FINE * a),
        )
    scaled_flat = scaled[:].rearrange("p c a -> p (c a)")
    turns = scratch.tile([P, CHUNKS * COARSE, FINE], F32)
    turns_flat = turns[:].rearrange("p r b -> p (r b)")
    whole = scratch.tile([P, ROW_PAIRS], F32)
    rows = CHUNKS * COARSE // BANKS
    banks = [slice(BANK_PAIRS * bank, BANK_PAIRS * (bank + 1)) for bank in range(BANKS)]
    for bank in range(BANKS):
        nc.vector.tensor_tensor(
            out=turns[:, rows * bank : rows * (bank + 1), :],
            in0=scaled_flat[:, rows * bank : rows * (bank + 1)]
            .unsqueeze(2)
            .to_broadcast([P, rows, FINE]),
            in1=fine[:].unsqueeze(1).to_broadcast([P, rows, FINE]),
            op=ALU.mult,
        )
    for pairs in banks:
        nc.vector.tensor_scalar(
            out=whole[:, pairs],
            in0=turns_flat[:, pairs],
            scalar1=ROUND_TO_WHOLE,
            scalar2=ROUND_TO_WHOLE,
            op0=ALU.add,
            op1=ALU.subtract,
        )
    for pairs in banks:
        nc.vector.tensor_tensor(
            out=part[:, pairs], in0=turns_flat[:, pairs], in1=whole[:, pairs], op=ALU.subtract
        )
    for pairs in banks:
        nc.vector.scalar_tensor_tensor(
            out=shifted[:, pairs],
            in0=part[:, pairs],
            scalar=0.25,
            in1=part[:, pairs],
            op0=ALU.is_gt,
            op1=ALU.subtract,
        )


def build_sines(nc, part, signed_sin, bank):
    pairs = slice(BANK_PAIRS * bank, BANK_PAIRS * bank + BANK_PAIRS)
    for sign in range(2):
        nc.scalar.activation(
            out=signed_sin[:, sign, pairs],
            in_=part[:, pairs],
            func=SIN,
            scale=(2 * sign - 1) * 2.0 * math.pi,
        )


def build_cosines(nc, shifted, cos, bank):
    pairs = slice(BANK_PAIRS * bank, BANK_PAIRS * bank + BANK_PAIRS)
    nc.scalar.activation(
        out=cos[:, pairs], in_=shifted[:, pairs], func=SIN, scale=-2.0 * math.pi, bias=math.pi / 2.0
    )


def tile_attention_pa_kernel(
    tc, emb, W1_words, W1_scales, W2_words, W2_scales, W3_words, W3_scales, out_0, out_1, out_2
):
    nc = tc.nc
    emb_rows = emb.rearrange("b s e -> (b s) e")
    weight_words = [W1_words, W2_words, W3_words]
    weight_scales = [W1_scales, W2_scales, W3_scales]
    out_rows = [
        out.rearrange("b h (s c) d -> (b h s) (c d)", c=CHUNKS) for out in (out_0, out_1, out_2)
    ]

    with ExitStack() as ctx:
        keep = ctx.enter_context(tc.tile_pool(name="keep", bufs=1))
        scratch = ctx.enter_context(tc.tile_pool(name="scratch", bufs=1))
        stage = ctx.enter_context(tc.tile_pool(name="stage", bufs=8))
        results = ctx.enter_context(tc.tile_pool(name="results", bufs=8))
        psum = ctx.enter_context(tc.psum_pool(name="psum", bufs=8))
        ctx.enter_context(tc.manual_schedule())

        x_sb = [keep.tile([P, FEATURES_IN], BF16, name="x_sb%d" % m) for m in range(TOKEN_TILES)]
        x_words = [
            keep.tile([P, PASSES * P], U32, align_bytes=64, name="x_words%d" % m)
            for m in range(TOKEN_TILES)
        ]
        x_scales = [
            keep.tile([P, PASSES * P], U8, align_bytes=64, name="x_scales%d" % m)
            for m in range(TOKEN_TILES)
        ]
        w_words = [
            [
                [
                    keep.tile([P, BANK], U32, align_bytes=64, name="w_words%d_%d_%d" % (w, bank, g))
                    for g in range(PASSES)
                ]
                for bank in range(BANKS)
            ]
            for w in range(WEIGHTS)
        ]
        w_planes = [
            keep.tile([P, FEATURES_OUT], U8, align_bytes=64, name="w_planes%d" % w)
            for w in range(WEIGHTS)
        ]

        def load_tokens(m):
            nc.sync.dma_start(out=x_sb[m][:], in_=emb_rows[P * m : P * m + P, :])

        def load_scales(w):
            for quadrant in range(QUADRANTS):
                rows = slice(32 * quadrant, 32 * quadrant + PASSES * 4)
                nc.sync.dma_start(
                    out=w_planes[w][rows, :].bitcast(I32),
                    in_=weight_scales[w][:, 4 * quadrant : 4 * quadrant + 4, :].bitcast(I32),
                )

        def load_words(w, bank):
            for g in range(PASSES):
                nc.sync.dma_start(
                    out=w_words[w][bank][g][:].bitcast(I32),
                    in_=weight_words[w][g]
                    .rearrange("p n t -> p (n t)")[:, PACK * BANK * bank : PACK * BANK * (bank + 1)]
                    .bitcast(I32),
                )

        position = scratch.tile([P, CHUNKS], F32)
        build_positions(nc, position)
        warm = scratch.tile([P, 2], F32)
        nc.gpsimd.memset(warm[:, 0:1], 0.0)
        nc.scalar.activation(out=warm[:, 1:2], in_=warm[:, 0:1], func=SIN)

        identity = keep.tile([P, P], F32)
        make_identity(nc, identity[:])
        for w in range(WEIGHTS):
            nc.gpsimd.memset(w_planes[w][:].bitcast(F32), 0.0)

        for m in range(TOKEN_TILES):
            load_tokens(m)
        for w in range(WEIGHTS):
            load_scales(w)
            for bank in range(BANKS):
                load_words(w, bank)

        part = scratch.tile([P, ROW_PAIRS], F32)
        shifted = scratch.tile([P, ROW_PAIRS], F32)
        cos = keep.tile([P, ROW_PAIRS], F32)
        signed_sin = keep.tile([P, 2, ROW_PAIRS], F32)
        build_angles(nc, scratch, position, part, shifted)

        grouped = {}

        def copies_of(m):
            if m == TOKEN_TILES - 1:
                return (((0,), nc.scalar.copy), ((1,), nc.vector.tensor_copy))
            if m in VECTOR_COPIES:
                return (((0, 1), nc.vector.tensor_copy),)
            return (((0, 1), nc.scalar.copy),)

        def turn_tokens(m):
            pair_words = x_sb[m][:].bitcast(F32)
            grouped[m] = stage.tile([P, PASSES * P * PACK], BF16, align_bytes=64, name="grouped")
            for passes, engine_copy in copies_of(m):
                flipped = psum.tile([P, len(passes), 2, P], F32, tag="bank")
                for i in range(len(passes)):
                    for u in range(2):
                        nc.tensor.transpose(
                            flipped[:, i, u, :],
                            pair_words[:, 256 * passes[i] + u : 256 * (passes[i] + 1) : 2],
                            identity[:],
                        )
                words = slice(2 * P * passes[0], 2 * P * (passes[-1] + 1))
                engine_copy(
                    out=grouped[m][:]
                    .bitcast(F32)[:, words]
                    .rearrange("p (g r u) -> p g r u", g=len(passes), u=2),
                    in_=flipped[:].rearrange("p g u r -> p g r u"),
                )

        def quantise_tokens(m):
            nc.vector.quantize_mx(
                out=x_words[m][:].bitcast(FP8X4), scales=x_scales[m][:], in_=grouped[m][:]
            )

        def project(acc, m, w, bank):
            columns = slice(BANK * bank, BANK * bank + BANK)
            for g in range(PASSES):
                nc.tensor.matmul_mx(
                    out=acc[:],
                    lhsT=x_words[m][:, P * g : P * g + P].bitcast(FP8X4),
                    lhsT_scale=x_scales[m][:, P * g : P * g + P],
                    rhs=w_words[w][bank][g][:].bitcast(FP8X4),
                    rhs_scale=w_planes[w][4 * g : P, columns],
                    start=(g == 0),
                    stop=(g == PASSES - 1),
                )

        def multiply_by_tables(m, w, bank, straight, crossed):
            acc = psum.tile([P, BANK], F32, tag="bank")
            project(acc, m, w, bank)
            x_pairs = acc[:].rearrange("p (j e) -> p j e", e=2)
            pairs = slice(BANK_PAIRS * bank, BANK_PAIRS * bank + BANK_PAIRS)
            nc.vector.tensor_tensor(
                out=straight[:, pairs, :],
                in0=x_pairs,
                in1=cos[:, pairs].unsqueeze(2).to_broadcast([P, BANK_PAIRS, 2]),
                op=ALU.mult,
            )
            nc.vector.tensor_tensor(
                out=crossed[:, pairs, :],
                in0=x_pairs[:, :, ::-1],
                in1=signed_sin[:, :, pairs].rearrange("p e j -> p j e"),
                op=ALU.mult,
            )

        def add_and_store(engine, m, w, start, width, straight, crossed):
            pairs = slice(start // 2, (start + width) // 2)
            engine.tensor_tensor(
                out=straight[:, pairs, :],
                in0=straight[:, pairs, :],
                in1=crossed[:, pairs, :],
                op=ALU.add,
            )
            nc.sync.dma_start(
                out=out_rows[w][P * m : P * m + P, start : start + width],
                in_=straight[:, pairs, :].rearrange("p j e -> p (j e)"),
            )

        def new_terms():
            straight = results.tile([P, ROW_PAIRS, 2], F32, name="straight")
            crossed = results.tile([P, ROW_PAIRS, 2], F32, name="crossed")
            return straight, crossed

        def rotated_bank(m, w, bank, terms):
            multiply_by_tables(m, w, bank, *terms)
            add_and_store(nc.gpsimd, m, w, BANK * bank, BANK, *terms)

        def rotated_product(m, w, gpsimd_banks):
            terms = new_terms()
            for bank in range(BANKS):
                multiply_by_tables(m, w, bank, *terms)
            add_and_store(nc.gpsimd, m, w, 0, BANK * gpsimd_banks, *terms)
            return terms

        def tensor_add_and_store(m, w, bank, terms):
            columns = slice(BANK * bank, BANK * bank + BANK)
            acc = psum.tile([P, BANK], F32, tag="bank")
            for i in range(len(terms)):
                nc.tensor.matmul(
                    acc[:],
                    lhsT=identity[:],
                    rhs=terms[i][:].rearrange("p j e -> p (j e)")[:, columns],
                    start=(i == 0),
                    stop=(i == len(terms) - 1),
                )
            summed = results.tile([P, BANK], F32)
            nc.scalar.copy(out=summed[:], in_=acc[:])
            nc.scalar.dma_start(out=out_rows[w][P * m : P * m + P, columns], in_=summed[:])

        def last_rotated_products(m):
            terms = new_terms()
            for bank in range(BANKS):
                rotated_bank(m, 0, bank, terms)
            plain_product(m - 1, ROTATED)
            plain_product(m, ROTATED)
            terms = new_terms()
            for bank in range(BANKS):
                multiply_by_tables(m, 1, bank, *terms)
            tensor_add_and_store(m - 1, 1, 1, waiting[m - 1])
            for start, width in ((0, BANK), (BANK, BANK // 2), (BANK + BANK // 2, BANK // 2)):
                add_and_store(nc.vector, m, 1, start, width, *terms)

        def plain_product(m, w):
            plain = results.tile([P, FEATURES_OUT], F32)
            for bank in range(BANKS):
                acc = psum.tile([P, BANK], F32, tag="bank")
                project(acc, m, w, bank)
                nc.scalar.copy(out=plain[:, BANK * bank : BANK * bank + BANK], in_=acc[:])
            nc.scalar.dma_start(out=out_rows[w][P * m : P * m + P, :], in_=plain[:])

        build_sines(nc, part, signed_sin, 0)
        for m in range(TOKEN_TILES):
            turn_tokens(m)
            if m == 0:
                build_cosines(nc, shifted, cos, 0)
            if m > 0:
                quantise_tokens(m - 1)
        quantise_tokens(TOKEN_TILES - 1)
        build_cosines(nc, shifted, cos, 1)
        build_sines(nc, part, signed_sin, 1)
        first_terms = [new_terms() for m in range(2)]
        rotated_bank(0, 0, 0, first_terms[0])
        rotated_bank(1, 0, 0, first_terms[1])
        rotated_bank(0, 0, 1, first_terms[0])
        rotated_product(0, 1, BANKS)
        rotated_bank(1, 0, 1, first_terms[1])
        rotated_product(1, 1, BANKS)
        plain_product(0, ROTATED)
        waiting = {}
        last = TOKEN_TILES - 1
        for m in range(2, last):
            rotated_product(m, 0, BANKS)
            plain_product(m - 1, ROTATED)
            if m in TENSOR_ADDS:
                waiting[m] = rotated_product(m, 1, 1)
            else:
                rotated_product(m, 1, BANKS)
            if m - 1 in TENSOR_ADDS:
                tensor_add_and_store(m - 1, 1, 1, waiting[m - 1])
        last_rotated_products(last)
